import numpy as np
import ml_dtypes

BF16 = ml_dtypes.bfloat16


def bf(x):
    return np.asarray(x, np.float32).astype(BF16)


def f32(x):
    return np.asarray(x, np.float32)


def f64(x):
    return np.asarray(x).astype(np.float64)


def striped(idx):
    return np.tile(idx.reshape(-1, 16).T, (8, 1))


R, H, S, N = 4, 256, 512, 256


def setup_inputs():
    return {"bmat": bf(2.0 * np.random.standard_normal((R * H, S)) / np.sqrt(H)), "x": bf(np.random.standard_normal((H, N))), "amat": f32(0.5 * np.random.standard_normal((R * H, N)) / np.sqrt(R)), "bias": f32(0.1 * np.random.standard_normal((H, N))), "offs": striped(np.random.permutation(S)[:N])}


def reference(bmat, x, amat, bias, offs):
    idx = offs[:16].T.reshape(-1)
    p = f64(bmat)[:, idx].reshape(R, H, N) * f64(x)[None, :, :]
    t = p.sum(axis=1)
    return (f64(amat).reshape(R, H, N) * t[:, None, :]).sum(axis=0) + f64(bias)

@@ -1,0 +1,56 @@
+import concourse.mybir as mybir
+
+R, H, S, N = 4, 256, 512, 256
+P = 128
+HB = H // P
+BF16, F32, U16 = mybir.dt.bfloat16, mybir.dt.float32, mybir.dt.uint16
+MULT, ADD = mybir.AluOpType.mult, mybir.AluOpType.add
+
+FLOPS = 2 * R * H * N + 2 * R * H * N + H * N
+BYTES = 2 * R * H * N + 2 * H * N + 4 * R * H * N + 4 * H * N + 2 * N + 4 * H * N
+
+
+def tile_translator_kernel(tc, bmat, x, amat, bias, offs, out):
+    nc = tc.nc
+    bmat_blocks = bmat.rearrange("(r kb p) s -> r kb p s", r=R, kb=HB, p=P)
+    x_blocks = x.rearrange("(kb p) j -> kb p j", kb=HB, p=P)
+    amat_ranks = amat.rearrange("(r hb p) j -> r p hb j", r=R, hb=HB, p=P)
+    bias_view = bias.rearrange("(hb p) j -> p hb j", hb=HB, p=P)
+    out_view = out.rearrange("(hb p) j -> p hb j", hb=HB, p=P)
+
+    with (
+        tc.tile_pool(name="held", bufs=1) as held,
+        tc.tile_pool(name="work", bufs=3) as work,
+        tc.psum_pool(name="psum", bufs=1) as psum,
+    ):
+        offsets = held.tile([P, N // 16], U16, name="offsets")
+        nc.sync.dma_start(offsets[:], offs)
+
+        windows = [[held.tile([P, S], BF16, name=f"window{r}_{kb}") for kb in range(HB)] for r in range(R)]
+        x_tiles = [held.tile([P, N], BF16, name=f"x{kb}") for kb in range(HB)]
+        up = [held.tile([P, HB, N], F32, name=f"up{r}") for r in range(R)]
+        acc = held.tile([P, HB, N], F32, name="acc")
+
+        loads = [(x_tiles[kb][:], x_blocks[kb]) for kb in range(HB)]
+        for r in range(R):
+            loads += [(windows[r][kb][:], bmat_blocks[r, kb]) for kb in range(HB)]
+            if r == 0:
+                loads.append((acc[:], bias_view))
+            loads.append((up[r][:], amat_ranks[r]))
+        for i, (tile_ap, dram_ap) in enumerate(loads):
+            (nc.scalar, nc.sync)[i % 2].dma_start(tile_ap, dram_ap)
+
+        ones = held.tile([P, P], BF16, name="ones")
+        nc.vector.memset(ones[:], 1.0)
+
+        for r in range(R):
+            t_all = psum.tile([P, N], F32, name=f"t_all{r}")
+            for kb in range(HB):
+                p = work.tile([P, N], BF16, name="p")
+                nc.vector.tensor_tensor(p[:], windows[r][kb][:].indirect(offsets[:]), x_tiles[kb][:], MULT)
+                nc.tensor.matmul(t_all[:], ones[:], p[:], start=(kb == 0), stop=(kb == HB - 1))
+            scaled = work.tile([P, HB, N], F32, name="scaled")
+            nc.vector.tensor_tensor(scaled[:], up[r][:], t_all[:].unsqueeze(1).to_broadcast([P, HB, N]), MULT)
+            nc.vector.tensor_tensor(acc[:], acc[:], scaled[:], ADD)
+
+        nc.sync.dma_start(out_view, acc[:])

@@ -1,4 +1,5 @@
 import concourse.mybir as mybir
+from concourse.masks import make_identity
 
 R, H, S, N = 4, 256, 512, 256
 P = 128
@@ -8,6 +9,10 @@ MULT, ADD = mybir.AluOpType.mult, mybir.AluOpType.add
 
 FLOPS = 2 * R * H * N + 2 * R * H * N + H * N
 BYTES = 2 * R * H * N + 2 * H * N + 4 * R * H * N + 4 * H * N + 2 * N + 4 * H * N
+
+
+def by_block(tile):
+    return tile[:].rearrange("p (hb j) -> p hb j", hb=HB)
 
 
 def tile_translator_kernel(tc, bmat, x, amat, bias, offs, out):
@@ -28,29 +33,51 @@ def tile_translator_kernel(tc, bmat, x, amat, bias, offs, out):
 
         windows = [[held.tile([P, S], BF16, name=f"window{r}_{kb}") for kb in range(HB)] for r in range(R)]
         x_tiles = [held.tile([P, N], BF16, name=f"x{kb}") for kb in range(HB)]
-        up = [held.tile([P, HB, N], F32, name=f"up{r}") for r in range(R)]
-        acc = held.tile([P, HB, N], F32, name="acc")
+        up = [held.tile([P, HB * N], F32, name=f"up{r}") for r in range(R)]
+        bias_tile = held.tile([P, HB * N], F32, name="bias_tile")
 
-        loads = [(x_tiles[kb][:], x_blocks[kb]) for kb in range(HB)]
+        loads = []
         for r in range(R):
-            loads += [(windows[r][kb][:], bmat_blocks[r, kb]) for kb in range(HB)]
-            if r == 0:
-                loads.append((acc[:], bias_view))
-            loads.append((up[r][:], amat_ranks[r]))
+            for kb in range(HB):
+                if r == 0:
+                    loads.append((x_tiles[kb][:], x_blocks[kb]))
+                loads.append((windows[r][kb][:], bmat_blocks[r, kb]))
+            if r == 1:
+                loads.append((by_block(bias_tile), bias_view))
+            if r >= 1:
+                loads.append((by_block(up[r - 1]), amat_ranks[r - 1]))
+        loads.append((by_block(up[R - 1]), amat_ranks[R - 1]))
         for i, (tile_ap, dram_ap) in enumerate(loads):
             (nc.scalar, nc.sync)[i % 2].dma_start(tile_ap, dram_ap)
 
         ones = held.tile([P, P], BF16, name="ones")
         nc.vector.memset(ones[:], 1.0)
+        identity = held.tile([P, P], F32, name="identity")
+        make_identity(nc, identity[:])
 
-        for r in range(R):
-            t_all = psum.tile([P, N], F32, name=f"t_all{r}")
+        t_all = [psum.tile([P, N], F32, name=f"t_all{r}") for r in range(R)]
+        acc = psum.tile([P, HB * N], F32, name="acc")
+        scaled = [None] * R
+
+        def down(r):
             for kb in range(HB):
                 p = work.tile([P, N], BF16, name="p")
                 nc.vector.tensor_tensor(p[:], windows[r][kb][:].indirect(offsets[:]), x_tiles[kb][:], MULT)
-                nc.tensor.matmul(t_all[:], ones[:], p[:], start=(kb == 0), stop=(kb == HB - 1))
-            scaled = work.tile([P, HB, N], F32, name="scaled")
-            nc.vector.tensor_tensor(scaled[:], up[r][:], t_all[:].unsqueeze(1).to_broadcast([P, HB, N]), MULT)
-            nc.vector.tensor_tensor(acc[:], acc[:], scaled[:], ADD)
+                nc.tensor.matmul(t_all[r][:], ones[:], p[:], start=(kb == 0), stop=(kb == HB - 1))
 
-        nc.sync.dma_start(out_view, acc[:])
+        def scale(r):
+            scaled[r] = work.tile([P, HB * N], F32, name="scaled")
+            nc.vector.tensor_tensor(
+                by_block(scaled[r]), by_block(up[r]), t_all[r][:].unsqueeze(1).to_broadcast([P, HB, N]), MULT
+            )
+
+        down(0)
+        nc.tensor.matmul(acc[:], identity[:], bias_tile[:], start=True, stop=False)
+        for r in range(1, R):
+            down(r)
+            scale(r - 1)
+            nc.tensor.matmul(acc[:], identity[:], scaled[r - 1][:], start=False, stop=(r == R - 1))
+        scale(R - 1)
+        result = held.tile([P, HB * N], F32, name="result")
+        nc.vector.tensor_tensor(result[:], scaled[R - 1][:], acc[:], ADD)
+        nc.sync.dma_start(out_view, by_block(result))

@@ -1,5 +1,4 @@
 import concourse.mybir as mybir
-from concourse.masks import make_identity
 
 R, H, S, N = 4, 256, 512, 256
 P = 128
@@ -21,11 +20,12 @@ def tile_translator_kernel(tc, bmat, x, amat, bias, offs, out):
     x_blocks = x.rearrange("(kb p) j -> kb p j", kb=HB, p=P)
     amat_ranks = amat.rearrange("(r hb p) j -> r p hb j", r=R, hb=HB, p=P)
     bias_view = bias.rearrange("(hb p) j -> p hb j", hb=HB, p=P)
-    out_view = out.rearrange("(hb p) j -> p hb j", hb=HB, p=P)
+    out_blocks = out.rearrange("(hb p) j -> hb p j", hb=HB, p=P)
 
     with (
         tc.tile_pool(name="held", bufs=1) as held,
-        tc.tile_pool(name="work", bufs=3) as work,
+        tc.tile_pool(name="work", bufs=4) as work,
+        tc.tile_pool(name="products", bufs=R * HB) as products,
         tc.psum_pool(name="psum", bufs=1) as psum,
     ):
         offsets = held.tile([P, N // 16], U16, name="offsets")
@@ -44,24 +44,19 @@ def tile_translator_kernel(tc, bmat, x, amat, bias, offs, out):
                 loads.append((windows[r][kb][:], bmat_blocks[r, kb]))
             if r == 1:
                 loads.append((by_block(bias_tile), bias_view))
-            if r >= 1:
-                loads.append((by_block(up[r - 1]), amat_ranks[r - 1]))
-        loads.append((by_block(up[R - 1]), amat_ranks[R - 1]))
+        loads += [(by_block(up[r]), amat_ranks[r]) for r in range(R)]
         for i, (tile_ap, dram_ap) in enumerate(loads):
             (nc.scalar, nc.sync)[i % 2].dma_start(tile_ap, dram_ap)
 
         ones = held.tile([P, P], BF16, name="ones")
         nc.vector.memset(ones[:], 1.0)
-        identity = held.tile([P, P], F32, name="identity")
-        make_identity(nc, identity[:])
 
         t_all = [psum.tile([P, N], F32, name=f"t_all{r}") for r in range(R)]
-        acc = psum.tile([P, HB * N], F32, name="acc")
         scaled = [None] * R
 
         def down(r):
             for kb in range(HB):
-                p = work.tile([P, N], BF16, name="p")
+                p = products.tile([P, N], BF16, name="p")
                 nc.vector.tensor_tensor(p[:], windows[r][kb][:].indirect(offsets[:]), x_tiles[kb][:], MULT)
                 nc.tensor.matmul(t_all[r][:], ones[:], p[:], start=(kb == 0), stop=(kb == HB - 1))
 
@@ -71,13 +66,19 @@ def tile_translator_kernel(tc, bmat, x, amat, bias, offs, out):
                 by_block(scaled[r]), by_block(up[r]), t_all[r][:].unsqueeze(1).to_broadcast([P, HB, N]), MULT
             )
 
-        down(0)
-        nc.tensor.matmul(acc[:], identity[:], bias_tile[:], start=True, stop=False)
-        for r in range(1, R):
+        for r in range(R):
             down(r)
-            scale(r - 1)
-            nc.tensor.matmul(acc[:], identity[:], scaled[r - 1][:], start=False, stop=(r == R - 1))
-        scale(R - 1)
-        result = held.tile([P, HB * N], F32, name="result")
-        nc.vector.tensor_tensor(result[:], scaled[R - 1][:], acc[:], ADD)
-        nc.sync.dma_start(out_view, by_block(result))
+        for r in range(R):
+            scale(r)
+            if r == 0:
+                nc.gpsimd.tensor_tensor(bias_tile[:], bias_tile[:], scaled[0][:], ADD)
+        middle = held.tile([P, HB * N], F32, name="middle")
+        nc.vector.tensor_tensor(middle[:], scaled[1][:], scaled[2][:], ADD)
+        blocks = [slice(hb * N, (hb + 1) * N) for hb in range(HB)]
+        outer = held.tile([P, HB * N], F32, name="outer")
+        for cols in blocks:
+            nc.vector.tensor_tensor(outer[:, cols], scaled[3][:, cols], bias_tile[:, cols], ADD)
+        for hb, cols in enumerate(blocks):
+            total = held.tile([P, N], F32, name=f"total{hb}")
+            nc.vector.tensor_tensor(total[:], middle[:, cols], outer[:, cols], ADD)
+            (nc.sync, nc.scalar)[hb].dma_start(out_blocks[hb], total[:])

@@ -42,9 +42,10 @@ def tile_translator_kernel(tc, bmat, x, amat, bias, offs, out):
                 if r == 0:
                     loads.append((x_tiles[kb][:], x_blocks[kb]))
                 loads.append((windows[r][kb][:], bmat_blocks[r, kb]))
-            if r == 1:
+        for r in range(R):
+            loads.append((by_block(up[r]), amat_ranks[r]))
+            if r == 0:
                 loads.append((by_block(bias_tile), bias_view))
-        loads += [(by_block(up[r]), amat_ranks[r]) for r in range(R)]
         for i, (tile_ap, dram_ap) in enumerate(loads):
             (nc.scalar, nc.sync)[i % 2].dma_start(tile_ap, dram_ap)
 

@@ -71,8 +71,7 @@ def tile_translator_kernel(tc, bmat, x, amat, bias, offs, out):
             down(r)
         for r in range(R):
             scale(r)
-            if r == 0:
-                nc.gpsimd.tensor_tensor(bias_tile[:], bias_tile[:], scaled[0][:], ADD)
+        nc.vector.tensor_tensor(bias_tile[:], bias_tile[:], scaled[0][:], ADD)
         middle = held.tile([P, HB * N], F32, name="middle")
         nc.vector.tensor_tensor(middle[:], scaled[1][:], scaled[2][:], ADD)
         blocks = [slice(hb * N, (hb + 1) * N) for hb in range(HB)]

@@ -10,75 +10,57 @@ FLOPS = 2 * R * H * N + 2 * R * H * N + H * N
 BYTES = 2 * R * H * N + 2 * H * N + 4 * R * H * N + 4 * H * N + 2 * N + 4 * H * N
 
 
-def by_block(tile):
-    return tile[:].rearrange("p (hb j) -> p hb j", hb=HB)
-
-
 def tile_translator_kernel(tc, bmat, x, amat, bias, offs, out):
     nc = tc.nc
     bmat_blocks = bmat.rearrange("(r kb p) s -> r kb p s", r=R, kb=HB, p=P)
     x_blocks = x.rearrange("(kb p) j -> kb p j", kb=HB, p=P)
     amat_ranks = amat.rearrange("(r hb p) j -> r p hb j", r=R, hb=HB, p=P)
-    bias_view = bias.rearrange("(hb p) j -> p hb j", hb=HB, p=P)
+    bias_blocks = bias.rearrange("(hb p) j -> p hb j", hb=HB, p=P)
     out_blocks = out.rearrange("(hb p) j -> hb p j", hb=HB, p=P)
 
-    with (
-        tc.tile_pool(name="held", bufs=1) as held,
-        tc.tile_pool(name="work", bufs=4) as work,
-        tc.tile_pool(name="products", bufs=R * HB) as products,
-        tc.psum_pool(name="psum", bufs=1) as psum,
-    ):
-        offsets = held.tile([P, N // 16], U16, name="offsets")
+    with tc.tile_pool(name="sbuf", bufs=1) as sbuf, tc.psum_pool(name="psum", bufs=1) as psum:
+        offsets = sbuf.tile([P, N // 16], U16, name="offsets")
         nc.sync.dma_start(offsets[:], offs)
 
-        windows = [[held.tile([P, S], BF16, name=f"window{r}_{kb}") for kb in range(HB)] for r in range(R)]
-        x_tiles = [held.tile([P, N], BF16, name=f"x{kb}") for kb in range(HB)]
-        up = [held.tile([P, HB * N], F32, name=f"up{r}") for r in range(R)]
-        bias_tile = held.tile([P, HB * N], F32, name="bias_tile")
+        windows = [[sbuf.tile([P, S], BF16, name=f"window{r}_{kb}") for kb in range(HB)] for r in range(R)]
+        x_tiles = [sbuf.tile([P, N], BF16, name=f"x{kb}") for kb in range(HB)]
+        up = [sbuf.tile([P, HB, N], F32, name=f"up{r}") for r in range(R)]
+        bias_tile = sbuf.tile([P, HB, N], F32, name="bias_tile")
 
         loads = []
         for r in range(R):
             for kb in range(HB):
                 if r == 0:
-                    loads.append((x_tiles[kb][:], x_blocks[kb]))
-                loads.append((windows[r][kb][:], bmat_blocks[r, kb]))
-        for r in range(R):
-            loads.append((by_block(up[r]), amat_ranks[r]))
-            if r == 0:
-                loads.append((by_block(bias_tile), bias_view))
-        for i, (tile_ap, dram_ap) in enumerate(loads):
-            (nc.scalar, nc.sync)[i % 2].dma_start(tile_ap, dram_ap)
+                    loads.append((x_tiles[kb], x_blocks[kb]))
+                loads.append((windows[r][kb], bmat_blocks[r, kb]))
+        loads.append((up[0], amat_ranks[0]))
+        loads.append((bias_tile, bias_blocks))
+        loads += [(up[r], amat_ranks[r]) for r in range(1, R)]
+        for i, (dst, src) in enumerate(loads):
+            (nc.sync, nc.scalar)[i % 2].dma_start(dst[:], src)
 
-        ones = held.tile([P, P], BF16, name="ones")
+        ones = sbuf.tile([P, P], BF16, name="ones")
         nc.vector.memset(ones[:], 1.0)
 
         t_all = [psum.tile([P, N], F32, name=f"t_all{r}") for r in range(R)]
-        scaled = [None] * R
-
-        def down(r):
+        for r in range(R):
             for kb in range(HB):
-                p = products.tile([P, N], BF16, name="p")
+                p = sbuf.tile([P, N], BF16, name=f"p{r}_{kb}")
                 nc.vector.tensor_tensor(p[:], windows[r][kb][:].indirect(offsets[:]), x_tiles[kb][:], MULT)
                 nc.tensor.matmul(t_all[r][:], ones[:], p[:], start=(kb == 0), stop=(kb == HB - 1))
 
-        def scale(r):
-            scaled[r] = work.tile([P, HB * N], F32, name="scaled")
-            nc.vector.tensor_tensor(
-                by_block(scaled[r]), by_block(up[r]), t_all[r][:].unsqueeze(1).to_broadcast([P, HB, N]), MULT
-            )
+        scaled = [sbuf.tile([P, HB, N], F32, name=f"scaled{r}") for r in range(R)]
+        for r in range(R):
+            nc.vector.tensor_tensor(scaled[r][:], up[r][:], t_all[r][:].unsqueeze(1).to_broadcast([P, HB, N]), MULT)
 
-        for r in range(R):
-            down(r)
-        for r in range(R):
-            scale(r)
-        nc.vector.tensor_tensor(bias_tile[:], bias_tile[:], scaled[0][:], ADD)
-        middle = held.tile([P, HB * N], F32, name="middle")
+        first = sbuf.tile([P, HB, N], F32, name="first")
+        nc.gpsimd.tensor_tensor(first[:], bias_tile[:], scaled[0][:], ADD)
+        middle = sbuf.tile([P, HB, N], F32, name="middle")
         nc.vector.tensor_tensor(middle[:], scaled[1][:], scaled[2][:], ADD)
-        blocks = [slice(hb * N, (hb + 1) * N) for hb in range(HB)]
-        outer = held.tile([P, HB * N], F32, name="outer")
-        for cols in blocks:
-            nc.vector.tensor_tensor(outer[:, cols], scaled[3][:, cols], bias_tile[:, cols], ADD)
-        for hb, cols in enumerate(blocks):
-            total = held.tile([P, N], F32, name=f"total{hb}")
-            nc.vector.tensor_tensor(total[:], middle[:, cols], outer[:, cols], ADD)
-            (nc.sync, nc.scalar)[hb].dma_start(out_blocks[hb], total[:])
+        outer = sbuf.tile([P, HB, N], F32, name="outer")
+        for hb in range(HB):
+            nc.vector.tensor_tensor(outer[:, hb, :], scaled[3][:, hb, :], first[:, hb, :], ADD)
+        for hb in range(HB):
+            total = sbuf.tile([P, N], F32, name=f"total{hb}")
+            nc.vector.tensor_tensor(total[:], middle[:, hb, :], outer[:, hb, :], ADD)
+            (nc.sync, nc.scalar)[hb % 2].dma_start(out_blocks[hb], total[:])

@@ -14,9 +14,9 @@ def tile_translator_kernel(tc, bmat, x, amat, bias, offs, out):
     nc = tc.nc
     bmat_blocks = bmat.rearrange("(r kb p) s -> r kb p s", r=R, kb=HB, p=P)
     x_blocks = x.rearrange("(kb p) j -> kb p j", kb=HB, p=P)
-    amat_ranks = amat.rearrange("(r hb p) j -> r p hb j", r=R, hb=HB, p=P)
-    bias_blocks = bias.rearrange("(hb p) j -> p hb j", hb=HB, p=P)
-    out_blocks = out.rearrange("(hb p) j -> hb p j", hb=HB, p=P)
+    amat_ranks = amat.rearrange("(r p hb) j -> r p hb j", r=R, hb=HB, p=P)
+    bias_blocks = bias.rearrange("(p hb) j -> p hb j", hb=HB, p=P)
+    out_blocks = out.rearrange("(p hb) j -> hb p j", hb=HB, p=P)
 
     with tc.tile_pool(name="sbuf", bufs=1) as sbuf, tc.psum_pool(name="psum", bufs=1) as psum:
         offsets = sbuf.tile([P, N // 16], U16, name="offsets")

@@ -3,8 +3,10 @@ import concourse.mybir as mybir
 R, H, S, N = 4, 256, 512, 256
 P = 128
 HB = H // P
+JB = N // P
 BF16, F32, U16 = mybir.dt.bfloat16, mybir.dt.float32, mybir.dt.uint16
-MULT, ADD = mybir.AluOpType.mult, mybir.AluOpType.add
+MULT, ADD, EQUAL = mybir.AluOpType.mult, mybir.AluOpType.add, mybir.AluOpType.is_equal
+COPY = mybir.ActivationFunctionType.Copy
 
 FLOPS = 2 * R * H * N + 2 * R * H * N + H * N
 BYTES = 2 * R * H * N + 2 * H * N + 4 * R * H * N + 4 * H * N + 2 * N + 4 * H * N
@@ -33,34 +35,72 @@ def tile_translator_kernel(tc, bmat, x, amat, bias, offs, out):
                 if r == 0:
                     loads.append((x_tiles[kb], x_blocks[kb]))
                 loads.append((windows[r][kb], bmat_blocks[r, kb]))
-        loads.append((up[0], amat_ranks[0]))
+            if r == R - 3:
+                loads.append((up[0], amat_ranks[0]))
+        loads.append((up[1], amat_ranks[1]))
         loads.append((bias_tile, bias_blocks))
-        loads += [(up[r], amat_ranks[r]) for r in range(1, R)]
+        loads += [(up[r], amat_ranks[r]) for r in range(2, R)]
         for i, (dst, src) in enumerate(loads):
             (nc.sync, nc.scalar)[i % 2].dma_start(dst[:], src)
 
         ones = sbuf.tile([P, P], BF16, name="ones")
         nc.vector.memset(ones[:], 1.0)
 
-        t_all = [psum.tile([P, N], F32, name=f"t_all{r}") for r in range(R)]
+        ones_f32 = sbuf.tile([P, P], F32, name="ones_f32")
+        nc.vector.memset(ones_f32[:], 1.0)
+        column = sbuf.tile([P, P], BF16, name="column")
+        nc.vector.tensor_tensor_scan(column[:], ones_f32[:], ones_f32[:], 0.0, MULT, ADD)
+        row_times_p = psum.tile([P, P], F32, name="row_times_p")
+        nc.tensor.matmul(row_times_p[:], column[:], ones[:], start=True, stop=True)
+        identity = sbuf.tile([P, P], F32, name="identity")
+        nc.vector.scalar_tensor_tensor(identity[:], column[:], float(P), row_times_p[:], MULT, EQUAL)
+
+        t_all = [psum.tile([P, N], F32, name=f"t_all{r}") for r in range(1, R)]
         for r in range(R):
+            p_tiles = []
             for kb in range(HB):
                 p = sbuf.tile([P, N], BF16, name=f"p{r}_{kb}")
                 nc.vector.tensor_tensor(p[:], windows[r][kb][:].indirect(offsets[:]), x_tiles[kb][:], MULT)
-                nc.tensor.matmul(t_all[r][:], ones[:], p[:], start=(kb == 0), stop=(kb == HB - 1))
+                p_tiles.append(p)
+                if r > 0:
+                    nc.tensor.matmul(t_all[r - 1][:], ones[:], p[:], start=(kb == 0), stop=(kb == HB - 1))
+            if r == 0:
+                t0_psum = psum.tile([P, JB], F32, name="t0_psum")
+                for jb in range(JB):
+                    for kb in range(HB):
+                        nc.tensor.matmul(
+                            t0_psum[:, jb : jb + 1], p_tiles[kb][:, jb * P : (jb + 1) * P], ones[:, 0:1],
+                            start=(kb == 0), stop=(kb == HB - 1),
+                        )
+                t0 = sbuf.tile([P, JB], F32, name="t0")
+                nc.scalar.copy(t0[:], t0_psum[:])
 
-        scaled = [sbuf.tile([P, HB, N], F32, name=f"scaled{r}") for r in range(R)]
-        for r in range(R):
-            nc.vector.tensor_tensor(scaled[r][:], up[r][:], t_all[r][:].unsqueeze(1).to_broadcast([P, HB, N]), MULT)
+        turned = psum.tile([P, JB, HB, P], F32, name="turned")
+        for jb in range(JB):
+            for hb in range(HB):
+                nc.tensor.transpose(turned[:, jb, hb, :], up[0][:, hb, jb * P : (jb + 1) * P], identity[:])
+        scaled_turned = sbuf.tile([P, JB, HB, P], F32, name="scaled_turned")
+        for jb in range(JB):
+            nc.scalar.activation(scaled_turned[:, jb], turned[:, jb], COPY, scale=t0[:, jb : jb + 1])
+        scaled0 = psum.tile([P, HB, N], F32, name="scaled0")
+        for jb in range(JB):
+            for hb in range(HB):
+                nc.tensor.transpose(scaled0[:, hb, jb * P : (jb + 1) * P], scaled_turned[:, jb, hb, :], identity[:])
+
+        scaled = [None] + [sbuf.tile([P, HB, N], F32, name=f"scaled{r}") for r in range(1, R)]
+        for r in range(1, R):
+            nc.vector.tensor_tensor(
+                scaled[r][:], up[r][:], t_all[r - 1][:].unsqueeze(1).to_broadcast([P, HB, N]), MULT
+            )
 
         first = sbuf.tile([P, HB, N], F32, name="first")
-        nc.gpsimd.tensor_tensor(first[:], bias_tile[:], scaled[0][:], ADD)
-        middle = sbuf.tile([P, HB, N], F32, name="middle")
-        nc.vector.tensor_tensor(middle[:], scaled[1][:], scaled[2][:], ADD)
+        nc.gpsimd.tensor_tensor(first[:], bias_tile[:], scaled[1][:], ADD)
+        inner = sbuf.tile([P, HB, N], F32, name="inner")
+        nc.vector.tensor_tensor(inner[:], scaled[2][:], scaled0[:], ADD)
         outer = sbuf.tile([P, HB, N], F32, name="outer")
         for hb in range(HB):
             nc.vector.tensor_tensor(outer[:, hb, :], scaled[3][:, hb, :], first[:, hb, :], ADD)
         for hb in range(HB):
             total = sbuf.tile([P, N], F32, name=f"total{hb}")
-            nc.vector.tensor_tensor(total[:], middle[:, hb, :], outer[:, hb, :], ADD)
+            nc.vector.tensor_tensor(total[:], inner[:, hb, :], outer[:, hb, :], ADD)
             (nc.sync, nc.scalar)[hb % 2].dma_start(out_blocks[hb], total[:])

@@ -4,6 +4,7 @@ R, H, S, N = 4, 256, 512, 256
 P = 128
 HB = H // P
 JB = N // P
+TURNED = 2
 BF16, F32, U16 = mybir.dt.bfloat16, mybir.dt.float32, mybir.dt.uint16
 MULT, ADD, EQUAL = mybir.AluOpType.mult, mybir.AluOpType.add, mybir.AluOpType.is_equal
 COPY = mybir.ActivationFunctionType.Copy
@@ -14,8 +15,8 @@ BYTES = 2 * R * H * N + 2 * H * N + 4 * R * H * N + 4 * H * N + 2 * N + 4 * H * 
 
 def tile_translator_kernel(tc, bmat, x, amat, bias, offs, out):
     nc = tc.nc
-    bmat_blocks = bmat.rearrange("(r kb p) s -> r kb p s", r=R, kb=HB, p=P)
-    x_blocks = x.rearrange("(kb p) j -> kb p j", kb=HB, p=P)
+    bmat_blocks = bmat.rearrange("(r p kb) s -> r kb p s", r=R, kb=HB, p=P)
+    x_rows = x.rearrange("(p kb) j -> p kb j", kb=HB, p=P)
     amat_ranks = amat.rearrange("(r p hb) j -> r p hb j", r=R, hb=HB, p=P)
     bias_blocks = bias.rearrange("(p hb) j -> p hb j", hb=HB, p=P)
     out_blocks = out.rearrange("(p hb) j -> hb p j", hb=HB, p=P)
@@ -25,21 +26,21 @@ def tile_translator_kernel(tc, bmat, x, amat, bias, offs, out):
         nc.sync.dma_start(offsets[:], offs)
 
         windows = [[sbuf.tile([P, S], BF16, name=f"window{r}_{kb}") for kb in range(HB)] for r in range(R)]
-        x_tiles = [sbuf.tile([P, N], BF16, name=f"x{kb}") for kb in range(HB)]
+        x_tile = sbuf.tile([P, HB, N], BF16, name="x_tile")
         up = [sbuf.tile([P, HB, N], F32, name=f"up{r}") for r in range(R)]
         bias_tile = sbuf.tile([P, HB, N], F32, name="bias_tile")
 
         loads = []
-        for r in range(R):
-            for kb in range(HB):
-                if r == 0:
-                    loads.append((x_tiles[kb], x_blocks[kb]))
-                loads.append((windows[r][kb], bmat_blocks[r, kb]))
-            if r == R - 3:
-                loads.append((up[0], amat_ranks[0]))
-        loads.append((up[1], amat_ranks[1]))
+        loads += [(x_tile, x_rows)]
+        loads += [(windows[0][kb], bmat_blocks[0, kb]) for kb in range(HB)]
+        for r in range(1, R):
+            loads.append((windows[r][0], bmat_blocks[r, 0]))
+            if r <= TURNED:
+                loads.append((up[r - 1], amat_ranks[r - 1]))
+            loads.append((windows[r][1], bmat_blocks[r, 1]))
+        loads.append((up[2], amat_ranks[2]))
         loads.append((bias_tile, bias_blocks))
-        loads += [(up[r], amat_ranks[r]) for r in range(2, R)]
+        loads.append((up[3], amat_ranks[3]))
         for i, (dst, src) in enumerate(loads):
             (nc.sync, nc.scalar)[i % 2].dma_start(dst[:], src)
 
@@ -55,51 +56,74 @@ def tile_translator_kernel(tc, bmat, x, amat, bias, offs, out):
         identity = sbuf.tile([P, P], F32, name="identity")
         nc.vector.scalar_tensor_tensor(identity[:], column[:], float(P), row_times_p[:], MULT, EQUAL)
 
-        t_all = [psum.tile([P, N], F32, name=f"t_all{r}") for r in range(1, R)]
-        for r in range(R):
-            p_tiles = []
+        turned_sum = psum.tile([P, HB, N], F32, name="turned_sum")
+        t_all, turned, t_scale, scaled_turned = {}, {}, {}, {}
+
+        def look_up(r, kb):
+            p = sbuf.tile([P, N], BF16, name=f"p{r}_{kb}")
+            nc.vector.tensor_tensor(p[:], windows[r][kb][:].indirect(offsets[:]), x_tile[:, kb, :], MULT)
+            return p
+
+        def sum_to_columns(r, p_tiles):
+            t_columns = psum.tile([P, JB], F32, name=f"t_columns{r}")
+            for jb in range(JB):
+                for kb in range(HB):
+                    nc.tensor.matmul(
+                        t_columns[:, jb : jb + 1], p_tiles[kb][:, jb * P : (jb + 1) * P], ones[:, 0:1],
+                        start=(kb == 0), stop=(kb == HB - 1),
+                    )
+            t_scale[r] = sbuf.tile([P, JB], F32, name=f"t_scale{r}")
+            nc.scalar.copy(t_scale[r][:], t_columns[:])
+
+        def turn(r):
+            turned[r] = psum.tile([P, JB, HB, P], F32, name=f"turned{r}")
+            for jb in range(JB):
+                for hb in range(HB):
+                    nc.tensor.transpose(turned[r][:, jb, hb, :], up[r][:, hb, jb * P : (jb + 1) * P], identity[:])
+
+        def scale(r):
+            scaled_turned[r] = sbuf.tile([P, JB, HB, P], F32, name=f"scaled_turned{r}")
+            for jb in range(JB):
+                nc.scalar.activation(scaled_turned[r][:, jb], turned[r][:, jb], COPY, scale=t_scale[r][:, jb : jb + 1])
+
+        def turn_back_and_add(r):
+            for jb in range(JB):
+                for hb in range(HB):
+                    nc.tensor.matmul(
+                        turned_sum[:, hb, jb * P : (jb + 1) * P], scaled_turned[r][:, jb, hb, :], identity[:],
+                        is_transpose=True,
+                        start=(r == 0 and jb == 0 and hb == 0),
+                        stop=(r == TURNED - 1 and jb == JB - 1 and hb == HB - 1),
+                    )
+
+        def sum_to_all(r, p_tiles):
+            t_all[r] = psum.tile([P, N], F32, name=f"t_all{r}")
             for kb in range(HB):
-                p = sbuf.tile([P, N], BF16, name=f"p{r}_{kb}")
-                nc.vector.tensor_tensor(p[:], windows[r][kb][:].indirect(offsets[:]), x_tiles[kb][:], MULT)
-                p_tiles.append(p)
-                if r > 0:
-                    nc.tensor.matmul(t_all[r - 1][:], ones[:], p[:], start=(kb == 0), stop=(kb == HB - 1))
-            if r == 0:
-                t0_psum = psum.tile([P, JB], F32, name="t0_psum")
-                for jb in range(JB):
-                    for kb in range(HB):
-                        nc.tensor.matmul(
-                            t0_psum[:, jb : jb + 1], p_tiles[kb][:, jb * P : (jb + 1) * P], ones[:, 0:1],
-                            start=(kb == 0), stop=(kb == HB - 1),
-                        )
-                t0 = sbuf.tile([P, JB], F32, name="t0")
-                nc.scalar.copy(t0[:], t0_psum[:])
+                nc.tensor.matmul(t_all[r][:], ones[:], p_tiles[kb][:], start=(kb == 0), stop=(kb == HB - 1))
 
-        turned = psum.tile([P, JB, HB, P], F32, name="turned")
-        for jb in range(JB):
-            for hb in range(HB):
-                nc.tensor.transpose(turned[:, jb, hb, :], up[0][:, hb, jb * P : (jb + 1) * P], identity[:])
-        scaled_turned = sbuf.tile([P, JB, HB, P], F32, name="scaled_turned")
-        for jb in range(JB):
-            nc.scalar.activation(scaled_turned[:, jb], turned[:, jb], COPY, scale=t0[:, jb : jb + 1])
-        scaled0 = psum.tile([P, HB, N], F32, name="scaled0")
-        for jb in range(JB):
-            for hb in range(HB):
-                nc.tensor.transpose(scaled0[:, hb, jb * P : (jb + 1) * P], scaled_turned[:, jb, hb, :], identity[:])
+        for r in range(R):
+            p_tiles = [look_up(r, kb) for kb in range(HB)]
+            if 1 <= r <= TURNED:
+                scale(r - 1)
+            if r < TURNED:
+                sum_to_columns(r, p_tiles)
+                turn(r)
+            else:
+                sum_to_all(r, p_tiles)
+            if r >= 2:
+                turn_back_and_add(r - 2)
 
-        scaled = [None] + [sbuf.tile([P, HB, N], F32, name=f"scaled{r}") for r in range(1, R)]
-        for r in range(1, R):
+        scaled = {r: sbuf.tile([P, HB, N], F32, name=f"scaled{r}") for r in range(TURNED, R)}
+        for r in range(TURNED, R):
             nc.vector.tensor_tensor(
-                scaled[r][:], up[r][:], t_all[r - 1][:].unsqueeze(1).to_broadcast([P, HB, N]), MULT
+                scaled[r][:], up[r][:], t_all[r][:].unsqueeze(1).to_broadcast([P, HB, N]), MULT
             )
 
-        first = sbuf.tile([P, HB, N], F32, name="first")
-        nc.gpsimd.tensor_tensor(first[:], bias_tile[:], scaled[1][:], ADD)
         inner = sbuf.tile([P, HB, N], F32, name="inner")
-        nc.vector.tensor_tensor(inner[:], scaled[2][:], scaled0[:], ADD)
+        nc.vector.tensor_tensor(inner[:], scaled[2][:], bias_tile[:], ADD)
         outer = sbuf.tile([P, HB, N], F32, name="outer")
         for hb in range(HB):
-            nc.vector.tensor_tensor(outer[:, hb, :], scaled[3][:, hb, :], first[:, hb, :], ADD)
+            nc.vector.tensor_tensor(outer[:, hb, :], scaled[3][:, hb, :], turned_sum[:, hb, :], ADD)
         for hb in range(HB):
             total = sbuf.tile([P, N], F32, name=f"total{hb}")
             nc.vector.tensor_tensor(total[:], inner[:, hb, :], outer[:, hb, :], ADD)

@@ -15,8 +15,8 @@ BYTES = 2 * R * H * N + 2 * H * N + 4 * R * H * N + 4 * H * N + 2 * N + 4 * H * 
 
 def tile_translator_kernel(tc, bmat, x, amat, bias, offs, out):
     nc = tc.nc
-    bmat_blocks = bmat.rearrange("(r p kb) s -> r kb p s", r=R, kb=HB, p=P)
-    x_rows = x.rearrange("(p kb) j -> p kb j", kb=HB, p=P)
+    bmat_blocks = bmat.rearrange("(r kb p) s -> r kb p s", r=R, kb=HB, p=P)
+    x_blocks = x.rearrange("(kb p) j -> kb p j", kb=HB, p=P)
     amat_ranks = amat.rearrange("(r p hb) j -> r p hb j", r=R, hb=HB, p=P)
     bias_blocks = bias.rearrange("(p hb) j -> p hb j", hb=HB, p=P)
     out_blocks = out.rearrange("(p hb) j -> hb p j", hb=HB, p=P)
@@ -26,18 +26,17 @@ def tile_translator_kernel(tc, bmat, x, amat, bias, offs, out):
         nc.sync.dma_start(offsets[:], offs)
 
         windows = [[sbuf.tile([P, S], BF16, name=f"window{r}_{kb}") for kb in range(HB)] for r in range(R)]
-        x_tile = sbuf.tile([P, HB, N], BF16, name="x_tile")
+        x_tiles = [sbuf.tile([P, N], BF16, name=f"x{kb}") for kb in range(HB)]
         up = [sbuf.tile([P, HB, N], F32, name=f"up{r}") for r in range(R)]
         bias_tile = sbuf.tile([P, HB, N], F32, name="bias_tile")
 
         loads = []
-        loads += [(x_tile, x_rows)]
-        loads += [(windows[0][kb], bmat_blocks[0, kb]) for kb in range(HB)]
+        for kb in range(HB):
+            loads += [(x_tiles[kb], x_blocks[kb]), (windows[0][kb], bmat_blocks[0, kb])]
         for r in range(1, R):
-            loads.append((windows[r][0], bmat_blocks[r, 0]))
+            loads += [(windows[r][kb], bmat_blocks[r, kb]) for kb in range(HB)]
             if r <= TURNED:
                 loads.append((up[r - 1], amat_ranks[r - 1]))
-            loads.append((windows[r][1], bmat_blocks[r, 1]))
         loads.append((up[2], amat_ranks[2]))
         loads.append((bias_tile, bias_blocks))
         loads.append((up[3], amat_ranks[3]))
@@ -61,7 +60,7 @@ def tile_translator_kernel(tc, bmat, x, amat, bias, offs, out):
 
         def look_up(r, kb):
             p = sbuf.tile([P, N], BF16, name=f"p{r}_{kb}")
-            nc.vector.tensor_tensor(p[:], windows[r][kb][:].indirect(offsets[:]), x_tile[:, kb, :], MULT)
+            nc.vector.tensor_tensor(p[:], windows[r][kb][:].indirect(offsets[:]), x_tiles[kb][:], MULT)
             return p
 
         def sum_to_columns(r, p_tiles):

@@ -4,7 +4,7 @@ R, H, S, N = 4, 256, 512, 256
 P = 128
 HB = H // P
 JB = N // P
-TURNED = 2
+TURNED = (1, 2)
 BF16, F32, U16 = mybir.dt.bfloat16, mybir.dt.float32, mybir.dt.uint16
 MULT, ADD, EQUAL = mybir.AluOpType.mult, mybir.AluOpType.add, mybir.AluOpType.is_equal
 COPY = mybir.ActivationFunctionType.Copy
@@ -35,9 +35,9 @@ def tile_translator_kernel(tc, bmat, x, amat, bias, offs, out):
             loads += [(x_tiles[kb], x_blocks[kb]), (windows[0][kb], bmat_blocks[0, kb])]
         for r in range(1, R):
             loads += [(windows[r][kb], bmat_blocks[r, kb]) for kb in range(HB)]
-            if r <= TURNED:
-                loads.append((up[r - 1], amat_ranks[r - 1]))
-        loads.append((up[2], amat_ranks[2]))
+            if r in TURNED:
+                loads.append((up[r], amat_ranks[r]))
+        loads.append((up[0], amat_ranks[0]))
         loads.append((bias_tile, bias_blocks))
         loads.append((up[3], amat_ranks[3]))
         for i, (dst, src) in enumerate(loads):
@@ -71,7 +71,7 @@ def tile_translator_kernel(tc, bmat, x, amat, bias, offs, out):
                         t_columns[:, jb : jb + 1], p_tiles[kb][:, jb * P : (jb + 1) * P], ones[:, 0:1],
                         start=(kb == 0), stop=(kb == HB - 1),
                     )
-            t_scale[r] = sbuf.tile([P, JB], F32, name=f"t_scale{r}")
+            t_scale[r] = sbuf.tile([P, JB], F32, name=f"t_scale{r}", tag="t_scale")
             nc.scalar.copy(t_scale[r][:], t_columns[:])
 
         def turn(r):
@@ -91,8 +91,8 @@ def tile_translator_kernel(tc, bmat, x, amat, bias, offs, out):
                     nc.tensor.matmul(
                         turned_sum[:, hb, jb * P : (jb + 1) * P], scaled_turned[r][:, jb, hb, :], identity[:],
                         is_transpose=True,
-                        start=(r == 0 and jb == 0 and hb == 0),
-                        stop=(r == TURNED - 1 and jb == JB - 1 and hb == HB - 1),
+                        start=(r == TURNED[0] and jb == 0 and hb == 0),
+                        stop=(r == TURNED[-1] and jb == JB - 1 and hb == HB - 1),
                     )
 
         def sum_to_all(r, p_tiles):
@@ -102,28 +102,26 @@ def tile_translator_kernel(tc, bmat, x, amat, bias, offs, out):
 
         for r in range(R):
             p_tiles = [look_up(r, kb) for kb in range(HB)]
-            if 1 <= r <= TURNED:
-                scale(r - 1)
-            if r < TURNED:
+            if r in TURNED:
                 sum_to_columns(r, p_tiles)
                 turn(r)
+                scale(r)
             else:
                 sum_to_all(r, p_tiles)
-            if r >= 2:
-                turn_back_and_add(r - 2)
+        for r in TURNED:
+            turn_back_and_add(r)
 
-        scaled = {r: sbuf.tile([P, HB, N], F32, name=f"scaled{r}") for r in range(TURNED, R)}
-        for r in range(TURNED, R):
-            nc.vector.tensor_tensor(
-                scaled[r][:], up[r][:], t_all[r][:].unsqueeze(1).to_broadcast([P, HB, N]), MULT
-            )
+        def up_step(name, in0, in1, op):
+            step = sbuf.tile([P, HB, N], F32, name=name)
+            for hb in range(HB):
+                nc.vector.tensor_tensor(step[:, hb, :], in0(hb), in1(hb), op)
+            return step
 
-        inner = sbuf.tile([P, HB, N], F32, name="inner")
-        nc.vector.tensor_tensor(inner[:], scaled[2][:], bias_tile[:], ADD)
-        outer = sbuf.tile([P, HB, N], F32, name="outer")
-        for hb in range(HB):
-            nc.vector.tensor_tensor(outer[:, hb, :], scaled[3][:, hb, :], turned_sum[:, hb, :], ADD)
+        scaled0 = up_step("scaled0", lambda hb: up[0][:, hb, :], lambda hb: t_all[0][:], MULT)
+        biased0 = up_step("biased0", lambda hb: scaled0[:, hb, :], lambda hb: bias_tile[:, hb, :], ADD)
+        scaled3 = up_step("scaled3", lambda hb: up[3][:, hb, :], lambda hb: t_all[3][:], MULT)
+        direct_sum = up_step("direct_sum", lambda hb: scaled3[:, hb, :], lambda hb: biased0[:, hb, :], ADD)
         for hb in range(HB):
             total = sbuf.tile([P, N], F32, name=f"total{hb}")
-            nc.vector.tensor_tensor(total[:], inner[:, hb, :], outer[:, hb, :], ADD)
+            nc.vector.tensor_tensor(total[:], direct_sum[:, hb, :], turned_sum[:, hb, :], ADD)
             (nc.sync, nc.scalar)[hb % 2].dma_start(out_blocks[hb], total[:])

import concourse.mybir as mybir

R, H, S, N = 4, 256, 512, 256
P = 128
HB = H // P
JB = N // P
TURNED = (1, 2)
BF16, F32, U16 = mybir.dt.bfloat16, mybir.dt.float32, mybir.dt.uint16
MULT, ADD, EQUAL = mybir.AluOpType.mult, mybir.AluOpType.add, mybir.AluOpType.is_equal
COPY = mybir.ActivationFunctionType.Copy

FLOPS = 2 * R * H * N + 2 * R * H * N + H * N
BYTES = 2 * R * H * N + 2 * H * N + 4 * R * H * N + 4 * H * N + 2 * N + 4 * H * N


def tile_translator_kernel(tc, bmat, x, amat, bias, offs, out):
    nc = tc.nc
    bmat_blocks = bmat.rearrange("(r kb p) s -> r kb p s", r=R, kb=HB, p=P)
    x_blocks = x.rearrange("(kb p) j -> kb p j", kb=HB, p=P)
    amat_ranks = amat.rearrange("(r p hb) j -> r p hb j", r=R, hb=HB, p=P)
    bias_blocks = bias.rearrange("(p hb) j -> p hb j", hb=HB, p=P)
    out_blocks = out.rearrange("(p hb) j -> hb p j", hb=HB, p=P)

    with tc.tile_pool(name="sbuf", bufs=1) as sbuf, tc.psum_pool(name="psum", bufs=1) as psum:
        offsets = sbuf.tile([P, N // 16], U16, name="offsets")
        nc.sync.dma_start(offsets[:], offs)

        windows = [[sbuf.tile([P, S], BF16, name=f"window{r}_{kb}") for kb in range(HB)] for r in range(R)]
        x_tiles = [sbuf.tile([P, N], BF16, name=f"x{kb}") for kb in range(HB)]
        up = [sbuf.tile([P, HB, N], F32, name=f"up{r}") for r in range(R)]
        bias_tile = sbuf.tile([P, HB, N], F32, name="bias_tile")

        loads = []
        for kb in range(HB):
            loads += [(x_tiles[kb], x_blocks[kb]), (windows[0][kb], bmat_blocks[0, kb])]
        for r in range(1, R):
            loads += [(windows[r][kb], bmat_blocks[r, kb]) for kb in range(HB)]
            if r in TURNED:
                loads.append((up[r], amat_ranks[r]))
        loads.append((up[0], amat_ranks[0]))
        loads.append((bias_tile, bias_blocks))
        loads.append((up[3], amat_ranks[3]))
        for i, (dst, src) in enumerate(loads):
            (nc.sync, nc.scalar)[i % 2].dma_start(dst[:], src)

        ones = sbuf.tile([P, P], BF16, name="ones")
        nc.vector.memset(ones[:], 1.0)

        ones_f32 = sbuf.tile([P, P], F32, name="ones_f32")
        nc.vector.memset(ones_f32[:], 1.0)
        column = sbuf.tile([P, P], BF16, name="column")
        nc.vector.tensor_tensor_scan(column[:], ones_f32[:], ones_f32[:], 0.0, MULT, ADD)
        row_times_p = psum.tile([P, P], F32, name="row_times_p")
        nc.tensor.matmul(row_times_p[:], column[:], ones[:], start=True, stop=True)
        identity = sbuf.tile([P, P], F32, name="identity")
        nc.vector.scalar_tensor_tensor(identity[:], column[:], float(P), row_times_p[:], MULT, EQUAL)

        turned_sum = psum.tile([P, HB, N], F32, name="turned_sum")
        t_all, turned, t_scale, scaled_turned = {}, {}, {}, {}

        def look_up(r, kb):
            p = sbuf.tile([P, N], BF16, name=f"p{r}_{kb}")
            nc.vector.tensor_tensor(p[:], windows[r][kb][:].indirect(offsets[:]), x_tiles[kb][:], MULT)
            return p

        def sum_to_columns(r, p_tiles):
            t_columns = psum.tile([P, JB], F32, name=f"t_columns{r}")
            for jb in range(JB):
                for kb in range(HB):
                    nc.tensor.matmul(
                        t_columns[:, jb : jb + 1], p_tiles[kb][:, jb * P : (jb + 1) * P], ones[:, 0:1],
                        start=(kb == 0), stop=(kb == HB - 1),
                    )
            t_scale[r] = sbuf.tile([P, JB], F32, name=f"t_scale{r}", tag="t_scale")
            nc.scalar.copy(t_scale[r][:], t_columns[:])

        def turn(r):
            turned[r] = psum.tile([P, JB, HB, P], F32, name=f"turned{r}")
            for jb in range(JB):
                for hb in range(HB):
                    nc.tensor.transpose(turned[r][:, jb, hb, :], up[r][:, hb, jb * P : (jb + 1) * P], identity[:])

        def scale(r):
            scaled_turned[r] = sbuf.tile([P, JB, HB, P], F32, name=f"scaled_turned{r}")
            for jb in range(JB):
                nc.scalar.activation(scaled_turned[r][:, jb], turned[r][:, jb], COPY, scale=t_scale[r][:, jb : jb + 1])

        def turn_back_and_add(r):
            for jb in range(JB):
                for hb in range(HB):
                    nc.tensor.matmul(
                        turned_sum[:, hb, jb * P : (jb + 1) * P], scaled_turned[r][:, jb, hb, :], identity[:],
                        is_transpose=True,
                        start=(r == TURNED[0] and jb == 0 and hb == 0),
                        stop=(r == TURNED[-1] and jb == JB - 1 and hb == HB - 1),
                    )

        def sum_to_all(r, p_tiles):
            t_all[r] = psum.tile([P, N], F32, name=f"t_all{r}")
            for kb in range(HB):
                nc.tensor.matmul(t_all[r][:], ones[:], p_tiles[kb][:], start=(kb == 0), stop=(kb == HB - 1))

        for r in range(R):
            p_tiles = [look_up(r, kb) for kb in range(HB)]
            if r in TURNED:
                sum_to_columns(r, p_tiles)
                turn(r)
                scale(r)
            else:
                sum_to_all(r, p_tiles)
        for r in TURNED:
            turn_back_and_add(r)

        def up_step(name, in0, in1, op):
            step = sbuf.tile([P, HB, N], F32, name=name)
            for hb in range(HB):
                nc.vector.tensor_tensor(step[:, hb, :], in0(hb), in1(hb), op)
            return step

        scaled0 = up_step("scaled0", lambda hb: up[0][:, hb, :], lambda hb: t_all[0][:], MULT)
        biased0 = up_step("biased0", lambda hb: scaled0[:, hb, :], lambda hb: bias_tile[:, hb, :], ADD)
        scaled3 = up_step("scaled3", lambda hb: up[3][:, hb, :], lambda hb: t_all[3][:], MULT)
        direct_sum = up_step("direct_sum", lambda hb: scaled3[:, hb, :], lambda hb: biased0[:, hb, :], ADD)
        for hb in range(HB):
            total = sbuf.tile([P, N], F32, name=f"total{hb}")
            nc.vector.tensor_tensor(total[:], direct_sum[:, hb, :], turned_sum[:, hb, :], ADD)
            (nc.sync, nc.scalar)[hb % 2].dma_start(out_blocks[hb], total[:])
